import numpy as np
import ml_dtypes


def mxq(x, axis, fmt="e4m3"):
    dtype, down = {"e4m3": (ml_dtypes.float8_e4m3fn, 7), "e5m2": (ml_dtypes.float8_e5m2, 14)}[fmt]
    v = np.moveaxis(np.asarray(x, np.float32).astype(ml_dtypes.bfloat16).astype(np.float64), axis, -1)
    blocks = v.reshape(v.shape[:-1] + (-1, 32))
    amax = np.abs(blocks).max(-1, keepdims=True)
    byte = np.maximum(np.where(amax > 0, np.frexp(amax)[1] - 1 + 127, 0) - down, 1)
    scale = np.exp2(byte - 127.0)
    codes = (blocks / scale).astype(np.float32).astype(dtype).astype(np.float64)
    return np.moveaxis((codes * scale).reshape(v.shape), -1, axis)


WIDE = False


def mx_kscale(k):
    if not WIDE:
        return np.ones(k)
    levels = np.array([10, -10, 5, -5, 0])
    a = np.random.permutation(np.resize(levels, k // 512 * 4)).reshape(k // 512, 4)
    idx = np.arange(k)
    return np.exp2(a[idx // 512, idx % 128 // 32])


BF16 = ml_dtypes.bfloat16


def bf(x):
    return np.asarray(x, np.float32).astype(BF16)


def f64(x):
    return np.asarray(x).astype(np.float64)


B, H, W, C, F, K, G, RR = 4, 64, 64, 512, 128, 3, 16, 4
KK = K * K
P = B * H * W


def setup_inputs():
    s = mx_kscale(C)
    return {"x": bf(np.random.standard_normal((B, H, W, C)) * s),
            "Wi": bf(np.random.standard_normal((C, F)) / np.sqrt(C) / s[:, None]),
            "bi": bf(np.random.standard_normal(F) * 0.3),
            "w_span": bf(np.random.standard_normal((B, H, W, KK * G)) * 0.7)}


def reference(x, Wi, bi, w_span):
    xi = ((mxq(f64(x).reshape(P, C), 1, "e4m3") @ mxq(f64(Wi), 0, "e4m3")) + f64(bi)).reshape(B, H, W, F)
    pad = (K - 1) // 2
    xp = np.pad(xi, ((0, 0), (pad, pad), (pad, pad), (0, 0)))
    patches = np.stack([xp[:, i:i + H, j:j + W, :] for i in range(K) for j in range(K)], axis=-2)
    patches = patches.reshape(B, H, W, G, F // G, KK)
    w = f64(w_span).reshape(B, H, W, G, KK)[:, :, :, :, None, :]
    return (w * patches).sum(-1).reshape(B, H, W, F)

@@ -1,0 +1,266 @@
+from contextlib import ExitStack
+
+import concourse.mybir as mybir
+from concourse.masks import make_identity
+
+F32 = mybir.dt.float32
+BF16 = mybir.dt.bfloat16
+U32 = mybir.dt.uint32
+U8 = mybir.dt.uint8
+FP8X4 = mybir.dt.float8_e4m3fn_x4
+ADD = mybir.AluOpType.add
+MULT = mybir.AluOpType.mult
+
+P = 128
+IMAGES, HEIGHT, WIDTH = 4, 64, 64
+C_IN = 512
+C_OUT = 128
+TAPS = 9
+GROUPS = 16
+GROUP_CH = C_OUT // GROUPS
+GROUP_LEN = GROUP_CH * TAPS
+FLAT = TAPS * C_OUT
+
+PAIRS = IMAGES // 2
+QUAD = 4
+QUADS_PER_PAIR = HEIGHT // QUAD
+STEPS = PAIRS * QUADS_PER_PAIR
+
+PAD = 8
+ROW_W = PAD + P
+ROWS = HEIGHT + 3
+
+BANK = 512
+BANK_TAPS = BANK // C_OUT
+BANK_STEP = 3 * C_OUT
+
+GP_CH = 88
+
+FLOPS = 2 * IMAGES * HEIGHT * WIDTH * C_OUT * (C_IN + TAPS)
+
+
+def tile_involution2d_pa_t_kernel(tc, x, Wi, bi, w_span, out):
+    nc = tc.nc
+    with ExitStack() as ctx:
+        const = ctx.enter_context(tc.tile_pool(name="const", bufs=1))
+        x_pool = ctx.enter_context(tc.tile_pool(name="x_pool", bufs=4))
+        w_pool = ctx.enter_context(tc.tile_pool(name="w_pool", bufs=5))
+        mx_pool = ctx.enter_context(tc.tile_pool(name="mx_pool", bufs=2))
+        prod_pool = ctx.enter_context(tc.tile_pool(name="prod_pool", bufs=3))
+        fold_pool = ctx.enter_context(tc.tile_pool(name="fold_pool", bufs=1))
+        out_pool = ctx.enter_context(tc.tile_pool(name="out_pool", bufs=3))
+        xt_psum = ctx.enter_context(tc.psum_pool(name="xt_psum", bufs=2))
+        xi_psum = ctx.enter_context(tc.psum_pool(name="xi_psum", bufs=1))
+        tap_psum = ctx.enter_context(tc.psum_pool(name="tap_psum", bufs=5))
+
+        x_tiles, w_tiles, grouped_tiles, code_tiles = {}, {}, {}, {}
+        prod_tiles, out_tiles, banks = {}, {}, {}
+
+        def place(step):
+            pair, quad = divmod(step, QUADS_PER_PAIR)
+            return pair, quad * QUAD
+
+        def load_x(step):
+            pair, row0 = place(step)
+            x_sb = x_pool.tile([P, QUAD, C_IN], BF16, name="x_sb")
+            for r in range(2):
+                nc.sync.dma_start(
+                    out=x_sb[r:P:2, :, :],
+                    in_=x[2 * pair + r, row0 : row0 + QUAD, :, :].rearrange("u v k -> v u k"),
+                )
+            x_tiles[step] = x_sb
+
+        def load_w(step):
+            pair, row0 = place(step)
+            w_sb = w_pool.tile([P, QUAD, GROUPS * TAPS], BF16, name="w_sb")
+            for r in range(2):
+                nc.sync.dma_start(
+                    out=w_sb[r:P:2, :, :],
+                    in_=w_span[2 * pair + r, row0 : row0 + QUAD, :, :].rearrange("u v q -> v u q"),
+                )
+            w_tiles[step] = w_sb
+
+        for step in range(3):
+            load_x(step)
+
+        ident = const.tile([P, P], F32, name="ident")
+        make_identity(nc, ident[:])
+
+        wi_raw = const.tile([P, 4, C_OUT], BF16, name="wi_raw")
+        nc.sync.dma_start(
+            out=wi_raw[:].rearrange("q (h e) c -> q h e c", e=2),
+            in_=Wi.rearrange("(h q e) c -> q h e c", h=2, e=2),
+        )
+        wi_grouped = const.tile([P, C_OUT, 4], BF16, name="wi_grouped", align_bytes=64)
+        nc.vector.tensor_copy(out=wi_grouped[:], in_=wi_raw[:].rearrange("q t c -> q c t"))
+        wi_codes = const.tile([P, C_OUT], U32, name="wi_codes", align_bytes=64)
+        wi_scales = const.tile([P, C_OUT], U8, name="wi_scales", align_bytes=64)
+        nc.vector.quantize_mx(
+            out=wi_codes[:].bitcast(FP8X4),
+            scales=wi_scales[:],
+            in_=wi_grouped[:].rearrange("q c t -> q (c t)"),
+        )
+
+        bias_bf = const.tile([P, 1], BF16, name="bias_bf")
+        with nc.allow_non_contiguous_dma(reason="one bias value to each partition, once"):
+            nc.sync.dma_start(out=bias_bf[:], in_=bi.rearrange("(c o) -> c o", o=1))
+        bias = const.tile([P, 1], F32, name="bias")
+        nc.vector.tensor_copy(out=bias[:], in_=bias_bf[:])
+
+        xi_pad = []
+        for pair in range(PAIRS):
+            xi_sb = const.tile([P, ROWS, ROW_W], F32, name="xi_pad%d" % pair)
+            nc.gpsimd.memset(xi_sb[:, :, 0:PAD], 0.0)
+            nc.gpsimd.memset(xi_sb[:, 0:1, PAD:ROW_W], 0.0)
+            nc.gpsimd.memset(xi_sb[:, HEIGHT + 1 : ROWS, PAD:ROW_W], 0.0)
+            xi_pad.append(xi_sb)
+
+        def transpose_x(step):
+            x_sb = x_tiles.pop(step)
+            grouped = mx_pool.tile([P, QUAD * P, 4], BF16, name="grouped", align_bytes=64)
+            words = (
+                grouped[:]
+                .rearrange("q n t -> q (n t)")
+                .bitcast(F32)
+                .rearrange("q (a u n h) -> q a u n h", a=2, u=2, h=2)
+            )
+            for a in range(2):
+                xt = xt_psum.tile([P, 2, 2, P], F32, name="xt")
+                for u in range(2):
+                    x_words = x_sb[:, 2 * a + u, :].bitcast(F32)
+                    for h in range(2):
+                        nc.tensor.transpose(
+                            out=xt[:, u, h, :],
+                            in_=x_words[:, h * P : (h + 1) * P],
+                            identity=ident[:],
+                        )
+                nc.scalar.copy(out=words[:, a], in_=xt[:].rearrange("q u h n -> q u n h"))
+            grouped_tiles[step] = grouped
+
+        def quantise_x(step):
+            grouped = grouped_tiles.pop(step)
+            codes = mx_pool.tile([P, QUAD * P], U32, name="codes", align_bytes=64)
+            scales = mx_pool.tile([P, QUAD * P], U8, name="scales", align_bytes=64)
+            nc.vector.quantize_mx(
+                out=codes[:].bitcast(FP8X4),
+                scales=scales[:],
+                in_=grouped[:].rearrange("q n t -> q (n t)"),
+            )
+            code_tiles[step] = (codes, scales)
+
+        def project(step):
+            pair, row0 = place(step)
+            codes, scales = code_tiles.pop(step)
+            xi_ps = xi_psum.tile([P, QUAD * P], F32, name="xi_ps")
+            nc.tensor.matmul_mx(
+                out=xi_ps[:],
+                lhsT=wi_codes[:].bitcast(FP8X4),
+                lhsT_scale=wi_scales[:],
+                rhs=codes[:].bitcast(FP8X4),
+                rhs_scale=scales[:],
+                start=True,
+                stop=True,
+            )
+            nc.scalar.activation(
+                out=xi_pad[pair][:, 1 + row0 : 1 + row0 + QUAD, PAD:ROW_W],
+                in_=xi_ps[:].rearrange("c (u n) -> c u n", u=QUAD),
+                func=mybir.ActivationFunctionType.Identity,
+                bias=bias[:, 0:1],
+                scale=1.0,
+            )
+
+        bank_order = [(pair, row) for pair in range(PAIRS) for row in range(-1, HEIGHT + 1)]
+
+        def build_bank(pair, row):
+            flat = xi_pad[pair][:].rearrange("c r n -> c (r n)")
+            bank = tap_psum.tile([P, BANK], F32, name="bank")
+            for s in range(BANK_TAPS):
+                first = (row + 1 + s // 3) * ROW_W + PAD + 2 * (s % 3 - 1)
+                nc.tensor.transpose(
+                    out=bank[:, s * C_OUT : (s + 1) * C_OUT],
+                    in_=flat[:, first : first + P],
+                    identity=ident[:],
+                )
+            banks[(pair, row)] = bank
+
+        def multiply(pair, row, w_row, prod_row):
+            for b in range(3):
+                g0 = min(BANK_STEP * (b - 1) + BANK, FLAT) // GROUP_LEN if b else 0
+                g1 = min(BANK_STEP * b + BANK, FLAT) // GROUP_LEN
+                first = GROUP_LEN * g0 - BANK_STEP * b
+                nc.vector.tensor_tensor(
+                    out=prod_row[:, GROUP_LEN * g0 : GROUP_LEN * g1].rearrange(
+                        "p (g j m) -> p g j m", j=GROUP_CH, m=TAPS
+                    ),
+                    in0=banks[(pair, row - 1 + b)][
+                        :, first : first + GROUP_LEN * (g1 - g0)
+                    ].rearrange("p (g j m) -> p g j m", j=GROUP_CH, m=TAPS),
+                    in1=w_row[:, TAPS * g0 : TAPS * g1]
+                    .rearrange("p (g m) -> p g m", m=TAPS)
+                    .unsqueeze(2)
+                    .to_broadcast([P, g1 - g0, GROUP_CH, TAPS]),
+                    op=MULT,
+                )
+            banks.pop((pair, row - 1))
+
+        def fold_on_gpsimd(step):
+            terms = prod_tiles[step][:].rearrange("p u (o m) -> p u o m", m=TAPS)[:, :, 0:GP_CH, :]
+            sum4 = fold_pool.tile([P, QUAD, GP_CH, 4], F32, name="sum4")
+            sum2 = fold_pool.tile([P, QUAD, GP_CH, 2], F32, name="sum2")
+            sum1 = fold_pool.tile([P, QUAD, GP_CH], F32, name="sum1")
+            nc.gpsimd.tensor_tensor(
+                out=sum4[:], in0=terms[:, :, :, 0:4], in1=terms[:, :, :, 4:8], op=ADD
+            )
+            nc.gpsimd.tensor_tensor(
+                out=sum2[:], in0=sum4[:, :, :, 0:2], in1=sum4[:, :, :, 2:4], op=ADD
+            )
+            nc.gpsimd.tensor_tensor(
+                out=sum1[:], in0=sum2[:, :, :, 0], in1=sum2[:, :, :, 1], op=ADD
+            )
+            nc.gpsimd.tensor_tensor(
+                out=out_tiles[step][:, :, 0:GP_CH], in0=sum1[:], in1=terms[:, :, :, 8], op=ADD
+            )
+
+        def fold_on_vector_and_store(step):
+            pair, row0 = place(step)
+            terms = prod_tiles.pop(step)[:].rearrange("p u (o m) -> p u o m", m=TAPS)
+            out_sb = out_tiles.pop(step)
+            nc.vector.tensor_reduce(
+                out=out_sb[:, :, GP_CH:C_OUT],
+                in_=terms[:, :, GP_CH:C_OUT, :],
+                axis=mybir.AxisListType.X,
+                op=ADD,
+            )
+            for r in range(2):
+                nc.sync.dma_start(
+                    out=out[2 * pair + r, row0 : row0 + QUAD, :, :].rearrange("u v o -> v u o"),
+                    in_=out_sb[r:P:2, :, :],
+                )
+
+        built = 0
+        for step in range(-3, STEPS):
+            if step + 3 < STEPS:
+                transpose_x(step + 3)
+            if 0 <= step + 6 < STEPS:
+                load_x(step + 6)
+            if 0 <= step + 2 < STEPS:
+                quantise_x(step + 2)
+                load_w(step + 2)
+            if 0 <= step + 1 < STEPS:
+                project(step + 1)
+            if step < 0:
+                continue
+            pair, row0 = place(step)
+            prod_tiles[step] = prod_pool.tile([P, QUAD, FLAT], F32, name="prod")
+            out_tiles[step] = out_pool.tile([P, QUAD, C_OUT], F32, name="out_sb")
+            w_sb = w_tiles.pop(step)
+            for u in range(QUAD):
+                wanted = bank_order.index((pair, row0 + u + 1)) + 1
+                while built <= min(wanted, len(bank_order) - 1):
+                    build_bank(*bank_order[built])
+                    built += 1
+                multiply(pair, row0 + u, w_sb[:, u, :], prod_tiles[step][:, u, :])
+                if u == 0 and step > 0:
+                    fold_on_vector_and_store(step - 1)
+            fold_on_gpsimd(step)
+        fold_on_vector_and_store(STEPS - 1)

@@ -34,7 +34,7 @@ BANK = 512
 BANK_TAPS = BANK // C_OUT
 BANK_STEP = 3 * C_OUT
 
-GP_CH = 88
+GP_CH = 72
 
 FLOPS = 2 * IMAGES * HEIGHT * WIDTH * C_OUT * (C_IN + TAPS)
 

@@ -34,7 +34,7 @@ BANK = 512
 BANK_TAPS = BANK // C_OUT
 BANK_STEP = 3 * C_OUT
 
-GP_CH = 72
+VECTOR_EVERY = 3
 
 FLOPS = 2 * IMAGES * HEIGHT * WIDTH * C_OUT * (C_IN + TAPS)
 
@@ -46,9 +46,9 @@ def tile_involution2d_pa_t_kernel(tc, x, Wi, bi, w_span, out):
         x_pool = ctx.enter_context(tc.tile_pool(name="x_pool", bufs=4))
         w_pool = ctx.enter_context(tc.tile_pool(name="w_pool", bufs=5))
         mx_pool = ctx.enter_context(tc.tile_pool(name="mx_pool", bufs=2))
-        prod_pool = ctx.enter_context(tc.tile_pool(name="prod_pool", bufs=3))
+        prod_pool = ctx.enter_context(tc.tile_pool(name="prod_pool", bufs=4))
         fold_pool = ctx.enter_context(tc.tile_pool(name="fold_pool", bufs=1))
-        out_pool = ctx.enter_context(tc.tile_pool(name="out_pool", bufs=3))
+        out_pool = ctx.enter_context(tc.tile_pool(name="out_pool", bufs=4))
         xt_psum = ctx.enter_context(tc.psum_pool(name="xt_psum", bufs=2))
         xi_psum = ctx.enter_context(tc.psum_pool(name="xi_psum", bufs=1))
         tap_psum = ctx.enter_context(tc.psum_pool(name="tap_psum", bufs=5))
@@ -203,11 +203,14 @@ def tile_involution2d_pa_t_kernel(tc, x, Wi, bi, w_span, out):
                 )
             banks.pop((pair, row - 1))
 
+        def summed_by_vector(step):
+            return (STEPS - 1 - step) % VECTOR_EVERY == 0
+
         def fold_on_gpsimd(step):
-            terms = prod_tiles[step][:].rearrange("p u (o m) -> p u o m", m=TAPS)[:, :, 0:GP_CH, :]
-            sum4 = fold_pool.tile([P, QUAD, GP_CH, 4], F32, name="sum4")
-            sum2 = fold_pool.tile([P, QUAD, GP_CH, 2], F32, name="sum2")
-            sum1 = fold_pool.tile([P, QUAD, GP_CH], F32, name="sum1")
+            terms = prod_tiles.pop(step)[:].rearrange("p u (o m) -> p u o m", m=TAPS)
+            sum4 = fold_pool.tile([P, QUAD, C_OUT, 4], F32, name="sum4")
+            sum2 = fold_pool.tile([P, QUAD, C_OUT, 2], F32, name="sum2")
+            sum1 = fold_pool.tile([P, QUAD, C_OUT], F32, name="sum1")
             nc.gpsimd.tensor_tensor(
                 out=sum4[:], in0=terms[:, :, :, 0:4], in1=terms[:, :, :, 4:8], op=ADD
             )
@@ -218,19 +221,20 @@ def tile_involution2d_pa_t_kernel(tc, x, Wi, bi, w_span, out):
                 out=sum1[:], in0=sum2[:, :, :, 0], in1=sum2[:, :, :, 1], op=ADD
             )
             nc.gpsimd.tensor_tensor(
-                out=out_tiles[step][:, :, 0:GP_CH], in0=sum1[:], in1=terms[:, :, :, 8], op=ADD
+                out=out_tiles[step][:], in0=sum1[:], in1=terms[:, :, :, 8], op=ADD
             )
 
-        def fold_on_vector_and_store(step):
-            pair, row0 = place(step)
-            terms = prod_tiles.pop(step)[:].rearrange("p u (o m) -> p u o m", m=TAPS)
-            out_sb = out_tiles.pop(step)
+        def fold_on_vector(step):
             nc.vector.tensor_reduce(
-                out=out_sb[:, :, GP_CH:C_OUT],
-                in_=terms[:, :, GP_CH:C_OUT, :],
+                out=out_tiles[step][:],
+                in_=prod_tiles.pop(step)[:].rearrange("p u (o m) -> p u o m", m=TAPS),
                 axis=mybir.AxisListType.X,
                 op=ADD,
             )
+
+        def store(step):
+            pair, row0 = place(step)
+            out_sb = out_tiles.pop(step)
             for r in range(2):
                 nc.sync.dma_start(
                     out=out[2 * pair + r, row0 : row0 + QUAD, :, :].rearrange("u v o -> v u o"),
@@ -261,6 +265,10 @@ def tile_involution2d_pa_t_kernel(tc, x, Wi, bi, w_span, out):
                     built += 1
                 multiply(pair, row0 + u, w_sb[:, u, :], prod_tiles[step][:, u, :])
                 if u == 0 and step > 0:
-                    fold_on_vector_and_store(step - 1)
-            fold_on_gpsimd(step)
-        fold_on_vector_and_store(STEPS - 1)
+                    if summed_by_vector(step - 1):
+                        fold_on_vector(step - 1)
+                    store(step - 1)
+            if not summed_by_vector(step):
+                fold_on_gpsimd(step)
+        fold_on_vector(STEPS - 1)
+        store(STEPS - 1)

@@ -35,6 +35,7 @@ BANK_TAPS = BANK // C_OUT
 BANK_STEP = 3 * C_OUT
 
 VECTOR_EVERY = 3
+PROD_BUFS = 4
 
 FLOPS = 2 * IMAGES * HEIGHT * WIDTH * C_OUT * (C_IN + TAPS)
 
@@ -42,13 +43,14 @@ FLOPS = 2 * IMAGES * HEIGHT * WIDTH * C_OUT * (C_IN + TAPS)
 def tile_involution2d_pa_t_kernel(tc, x, Wi, bi, w_span, out):
     nc = tc.nc
     with ExitStack() as ctx:
+        ctx.enter_context(tc.manual_schedule())
         const = ctx.enter_context(tc.tile_pool(name="const", bufs=1))
         x_pool = ctx.enter_context(tc.tile_pool(name="x_pool", bufs=4))
         w_pool = ctx.enter_context(tc.tile_pool(name="w_pool", bufs=5))
         mx_pool = ctx.enter_context(tc.tile_pool(name="mx_pool", bufs=2))
-        prod_pool = ctx.enter_context(tc.tile_pool(name="prod_pool", bufs=4))
+        prod_pool = ctx.enter_context(tc.tile_pool(name="prod_pool", bufs=PROD_BUFS))
         fold_pool = ctx.enter_context(tc.tile_pool(name="fold_pool", bufs=1))
-        out_pool = ctx.enter_context(tc.tile_pool(name="out_pool", bufs=4))
+        out_pool = ctx.enter_context(tc.tile_pool(name="out_pool", bufs=PROD_BUFS + 2))
         xt_psum = ctx.enter_context(tc.psum_pool(name="xt_psum", bufs=2))
         xi_psum = ctx.enter_context(tc.psum_pool(name="xi_psum", bufs=1))
         tap_psum = ctx.enter_context(tc.psum_pool(name="tap_psum", bufs=5))
@@ -247,9 +249,10 @@ def tile_involution2d_pa_t_kernel(tc, x, Wi, bi, w_span, out):
                 transpose_x(step + 3)
             if 0 <= step + 6 < STEPS:
                 load_x(step + 6)
+            if 0 <= step + 3 < STEPS:
+                load_w(step + 3)
             if 0 <= step + 2 < STEPS:
                 quantise_x(step + 2)
-                load_w(step + 2)
             if 0 <= step + 1 < STEPS:
                 project(step + 1)
             if step < 0:
@@ -264,11 +267,12 @@ def tile_involution2d_pa_t_kernel(tc, x, Wi, bi, w_span, out):
                     build_bank(*bank_order[built])
                     built += 1
                 multiply(pair, row0 + u, w_sb[:, u, :], prod_tiles[step][:, u, :])
-                if u == 0 and step > 0:
-                    if summed_by_vector(step - 1):
-                        fold_on_vector(step - 1)
-                    store(step - 1)
+                if u == 0 and step > 0 and summed_by_vector(step - 1):
+                    fold_on_vector(step - 1)
             if not summed_by_vector(step):
                 fold_on_gpsimd(step)
+            if step >= PROD_BUFS:
+                store(step - PROD_BUFS)
         fold_on_vector(STEPS - 1)
-        store(STEPS - 1)
+        for step in range(STEPS - PROD_BUFS, STEPS):
+            store(step)

from contextlib import ExitStack

import concourse.mybir as mybir
from concourse.masks import make_identity

F32 = mybir.dt.float32
BF16 = mybir.dt.bfloat16
U32 = mybir.dt.uint32
U8 = mybir.dt.uint8
FP8X4 = mybir.dt.float8_e4m3fn_x4
ADD = mybir.AluOpType.add
MULT = mybir.AluOpType.mult

P = 128
IMAGES, HEIGHT, WIDTH = 4, 64, 64
C_IN = 512
C_OUT = 128
TAPS = 9
GROUPS = 16
GROUP_CH = C_OUT // GROUPS
GROUP_LEN = GROUP_CH * TAPS
FLAT = TAPS * C_OUT

PAIRS = IMAGES // 2
QUAD = 4
QUADS_PER_PAIR = HEIGHT // QUAD
STEPS = PAIRS * QUADS_PER_PAIR

PAD = 8
ROW_W = PAD + P
ROWS = HEIGHT + 3

BANK = 512
BANK_TAPS = BANK // C_OUT
BANK_STEP = 3 * C_OUT

VECTOR_EVERY = 3
PROD_BUFS = 4

FLOPS = 2 * IMAGES * HEIGHT * WIDTH * C_OUT * (C_IN + TAPS)


def tile_involution2d_pa_t_kernel(tc, x, Wi, bi, w_span, out):
    nc = tc.nc
    with ExitStack() as ctx:
        ctx.enter_context(tc.manual_schedule())
        const = ctx.enter_context(tc.tile_pool(name="const", bufs=1))
        x_pool = ctx.enter_context(tc.tile_pool(name="x_pool", bufs=4))
        w_pool = ctx.enter_context(tc.tile_pool(name="w_pool", bufs=5))
        mx_pool = ctx.enter_context(tc.tile_pool(name="mx_pool", bufs=2))
        prod_pool = ctx.enter_context(tc.tile_pool(name="prod_pool", bufs=PROD_BUFS))
        fold_pool = ctx.enter_context(tc.tile_pool(name="fold_pool", bufs=1))
        out_pool = ctx.enter_context(tc.tile_pool(name="out_pool", bufs=PROD_BUFS + 2))
        xt_psum = ctx.enter_context(tc.psum_pool(name="xt_psum", bufs=2))
        xi_psum = ctx.enter_context(tc.psum_pool(name="xi_psum", bufs=1))
        tap_psum = ctx.enter_context(tc.psum_pool(name="tap_psum", bufs=5))

        x_tiles, w_tiles, grouped_tiles, code_tiles = {}, {}, {}, {}
        prod_tiles, out_tiles, banks = {}, {}, {}

        def place(step):
            pair, quad = divmod(step, QUADS_PER_PAIR)
            return pair, quad * QUAD

        def load_x(step):
            pair, row0 = place(step)
            x_sb = x_pool.tile([P, QUAD, C_IN], BF16, name="x_sb")
            for r in range(2):
                nc.sync.dma_start(
                    out=x_sb[r:P:2, :, :],
                    in_=x[2 * pair + r, row0 : row0 + QUAD, :, :].rearrange("u v k -> v u k"),
                )
            x_tiles[step] = x_sb

        def load_w(step):
            pair, row0 = place(step)
            w_sb = w_pool.tile([P, QUAD, GROUPS * TAPS], BF16, name="w_sb")
            for r in range(2):
                nc.sync.dma_start(
                    out=w_sb[r:P:2, :, :],
                    in_=w_span[2 * pair + r, row0 : row0 + QUAD, :, :].rearrange("u v q -> v u q"),
                )
            w_tiles[step] = w_sb

        for step in range(3):
            load_x(step)

        ident = const.tile([P, P], F32, name="ident")
        make_identity(nc, ident[:])

        wi_raw = const.tile([P, 4, C_OUT], BF16, name="wi_raw")
        nc.sync.dma_start(
            out=wi_raw[:].rearrange("q (h e) c -> q h e c", e=2),
            in_=Wi.rearrange("(h q e) c -> q h e c", h=2, e=2),
        )
        wi_grouped = const.tile([P, C_OUT, 4], BF16, name="wi_grouped", align_bytes=64)
        nc.vector.tensor_copy(out=wi_grouped[:], in_=wi_raw[:].rearrange("q t c -> q c t"))
        wi_codes = const.tile([P, C_OUT], U32, name="wi_codes", align_bytes=64)
        wi_scales = const.tile([P, C_OUT], U8, name="wi_scales", align_bytes=64)
        nc.vector.quantize_mx(
            out=wi_codes[:].bitcast(FP8X4),
            scales=wi_scales[:],
            in_=wi_grouped[:].rearrange("q c t -> q (c t)"),
        )

        bias_bf = const.tile([P, 1], BF16, name="bias_bf")
        with nc.allow_non_contiguous_dma(reason="one bias value to each partition, once"):
            nc.sync.dma_start(out=bias_bf[:], in_=bi.rearrange("(c o) -> c o", o=1))
        bias = const.tile([P, 1], F32, name="bias")
        nc.vector.tensor_copy(out=bias[:], in_=bias_bf[:])

        xi_pad = []
        for pair in range(PAIRS):
            xi_sb = const.tile([P, ROWS, ROW_W], F32, name="xi_pad%d" % pair)
            nc.gpsimd.memset(xi_sb[:, :, 0:PAD], 0.0)
            nc.gpsimd.memset(xi_sb[:, 0:1, PAD:ROW_W], 0.0)
            nc.gpsimd.memset(xi_sb[:, HEIGHT + 1 : ROWS, PAD:ROW_W], 0.0)
            xi_pad.append(xi_sb)

        def transpose_x(step):
            x_sb = x_tiles.pop(step)
            grouped = mx_pool.tile([P, QUAD * P, 4], BF16, name="grouped", align_bytes=64)
            words = (
                grouped[:]
                .rearrange("q n t -> q (n t)")
                .bitcast(F32)
                .rearrange("q (a u n h) -> q a u n h", a=2, u=2, h=2)
            )
            for a in range(2):
                xt = xt_psum.tile([P, 2, 2, P], F32, name="xt")
                for u in range(2):
                    x_words = x_sb[:, 2 * a + u, :].bitcast(F32)
                    for h in range(2):
                        nc.tensor.transpose(
                            out=xt[:, u, h, :],
                            in_=x_words[:, h * P : (h + 1) * P],
                            identity=ident[:],
                        )
                nc.scalar.copy(out=words[:, a], in_=xt[:].rearrange("q u h n -> q u n h"))
            grouped_tiles[step] = grouped

        def quantise_x(step):
            grouped = grouped_tiles.pop(step)
            codes = mx_pool.tile([P, QUAD * P], U32, name="codes", align_bytes=64)
            scales = mx_pool.tile([P, QUAD * P], U8, name="scales", align_bytes=64)
            nc.vector.quantize_mx(
                out=codes[:].bitcast(FP8X4),
                scales=scales[:],
                in_=grouped[:].rearrange("q n t -> q (n t)"),
            )
            code_tiles[step] = (codes, scales)

        def project(step):
            pair, row0 = place(step)
            codes, scales = code_tiles.pop(step)
            xi_ps = xi_psum.tile([P, QUAD * P], F32, name="xi_ps")
            nc.tensor.matmul_mx(
                out=xi_ps[:],
                lhsT=wi_codes[:].bitcast(FP8X4),
                lhsT_scale=wi_scales[:],
                rhs=codes[:].bitcast(FP8X4),
                rhs_scale=scales[:],
                start=True,
                stop=True,
            )
            nc.scalar.activation(
                out=xi_pad[pair][:, 1 + row0 : 1 + row0 + QUAD, PAD:ROW_W],
                in_=xi_ps[:].rearrange("c (u n) -> c u n", u=QUAD),
                func=mybir.ActivationFunctionType.Identity,
                bias=bias[:, 0:1],
                scale=1.0,
            )

        bank_order = [(pair, row) for pair in range(PAIRS) for row in range(-1, HEIGHT + 1)]

        def build_bank(pair, row):
            flat = xi_pad[pair][:].rearrange("c r n -> c (r n)")
            bank = tap_psum.tile([P, BANK], F32, name="bank")
            for s in range(BANK_TAPS):
                first = (row + 1 + s // 3) * ROW_W + PAD + 2 * (s % 3 - 1)
                nc.tensor.transpose(
                    out=bank[:, s * C_OUT : (s + 1) * C_OUT],
                    in_=flat[:, first : first + P],
                    identity=ident[:],
                )
            banks[(pair, row)] = bank

        def multiply(pair, row, w_row, prod_row):
            for b in range(3):
                g0 = min(BANK_STEP * (b - 1) + BANK, FLAT) // GROUP_LEN if b else 0
                g1 = min(BANK_STEP * b + BANK, FLAT) // GROUP_LEN
                first = GROUP_LEN * g0 - BANK_STEP * b
                nc.vector.tensor_tensor(
                    out=prod_row[:, GROUP_LEN * g0 : GROUP_LEN * g1].rearrange(
                        "p (g j m) -> p g j m", j=GROUP_CH, m=TAPS
                    ),
                    in0=banks[(pair, row - 1 + b)][
                        :, first : first + GROUP_LEN * (g1 - g0)
                    ].rearrange("p (g j m) -> p g j m", j=GROUP_CH, m=TAPS),
                    in1=w_row[:, TAPS * g0 : TAPS * g1]
                    .rearrange("p (g m) -> p g m", m=TAPS)
                    .unsqueeze(2)
                    .to_broadcast([P, g1 - g0, GROUP_CH, TAPS]),
                    op=MULT,
                )
            banks.pop((pair, row - 1))

        def summed_by_vector(step):
            return (STEPS - 1 - step) % VECTOR_EVERY == 0

        def fold_on_gpsimd(step):
            terms = prod_tiles.pop(step)[:].rearrange("p u (o m) -> p u o m", m=TAPS)
            sum4 = fold_pool.tile([P, QUAD, C_OUT, 4], F32, name="sum4")
            sum2 = fold_pool.tile([P, QUAD, C_OUT, 2], F32, name="sum2")
            sum1 = fold_pool.tile([P, QUAD, C_OUT], F32, name="sum1")
            nc.gpsimd.tensor_tensor(
                out=sum4[:], in0=terms[:, :, :, 0:4], in1=terms[:, :, :, 4:8], op=ADD
            )
            nc.gpsimd.tensor_tensor(
                out=sum2[:], in0=sum4[:, :, :, 0:2], in1=sum4[:, :, :, 2:4], op=ADD
            )
            nc.gpsimd.tensor_tensor(
                out=sum1[:], in0=sum2[:, :, :, 0], in1=sum2[:, :, :, 1], op=ADD
            )
            nc.gpsimd.tensor_tensor(
                out=out_tiles[step][:], in0=sum1[:], in1=terms[:, :, :, 8], op=ADD
            )

        def fold_on_vector(step):
            nc.vector.tensor_reduce(
                out=out_tiles[step][:],
                in_=prod_tiles.pop(step)[:].rearrange("p u (o m) -> p u o m", m=TAPS),
                axis=mybir.AxisListType.X,
                op=ADD,
            )

        def store(step):
            pair, row0 = place(step)
            out_sb = out_tiles.pop(step)
            for r in range(2):
                nc.sync.dma_start(
                    out=out[2 * pair + r, row0 : row0 + QUAD, :, :].rearrange("u v o -> v u o"),
                    in_=out_sb[r:P:2, :, :],
                )

        built = 0
        for step in range(-3, STEPS):
            if step + 3 < STEPS:
                transpose_x(step + 3)
            if 0 <= step + 6 < STEPS:
                load_x(step + 6)
            if 0 <= step + 3 < STEPS:
                load_w(step + 3)
            if 0 <= step + 2 < STEPS:
                quantise_x(step + 2)
            if 0 <= step + 1 < STEPS:
                project(step + 1)
            if step < 0:
                continue
            pair, row0 = place(step)
            prod_tiles[step] = prod_pool.tile([P, QUAD, FLAT], F32, name="prod")
            out_tiles[step] = out_pool.tile([P, QUAD, C_OUT], F32, name="out_sb")
            w_sb = w_tiles.pop(step)
            for u in range(QUAD):
                wanted = bank_order.index((pair, row0 + u + 1)) + 1
                while built <= min(wanted, len(bank_order) - 1):
                    build_bank(*bank_order[built])
                    built += 1
                multiply(pair, row0 + u, w_sb[:, u, :], prod_tiles[step][:, u, :])
                if u == 0 and step > 0 and summed_by_vector(step - 1):
                    fold_on_vector(step - 1)
            if not summed_by_vector(step):
                fold_on_gpsimd(step)
            if step >= PROD_BUFS:
                store(step - PROD_BUFS)
        fold_on_vector(STEPS - 1)
        for step in range(STEPS - PROD_BUFS, STEPS):
            store(step)
